import numpy as np
import ml_dtypes


def mxq(x, axis, fmt="e4m3"):
    dtype, down = {"e4m3": (ml_dtypes.float8_e4m3fn, 7), "e5m2": (ml_dtypes.float8_e5m2, 14)}[fmt]
    v = np.moveaxis(np.asarray(x, np.float32).astype(ml_dtypes.bfloat16).astype(np.float64), axis, -1)
    blocks = v.reshape(v.shape[:-1] + (-1, 32))
    amax = np.abs(blocks).max(-1, keepdims=True)
    byte = np.maximum(np.where(amax > 0, np.frexp(amax)[1] - 1 + 127, 0) - down, 1)
    scale = np.exp2(byte - 127.0)
    codes = (blocks / scale).astype(np.float32).astype(dtype).astype(np.float64)
    return np.moveaxis((codes * scale).reshape(v.shape), -1, axis)


WIDE = False


def mx_kscale(k):
    if not WIDE:
        return np.ones(k)
    levels = np.array([30, -30])
    if k % 512:
        return np.exp2(np.random.permutation(np.resize(levels, k // 32))).repeat(32)
    a = np.empty((k // 512, 16))
    for p in range(k // 512):
        a[p, :8] = np.random.permutation(np.resize(levels, 8))
        for g in range(8):
            far = levels[np.abs(levels - a[p, g]) >= 10]
            a[p, g + 8] = far[np.random.randint(len(far))]
    return np.exp2(a.ravel()).repeat(32)


BF16 = ml_dtypes.bfloat16


def bf(x):
    return np.asarray(x, np.float32).astype(BF16)


def f64(x):
    return np.asarray(x).astype(np.float64)


B, L, H, D = 2, 512, 8, 128
DIM = H * D


def setup_inputs():
    r = np.random.standard_normal
    s = mx_kscale(DIM)
    ang = np.arange(L)[:, None, None] * (r((H, D)) * 0.2)[None]
    return {"x": bf(r((B, L, DIM)) * s),
            "wq_w": bf(r((DIM, DIM)) * 0.5 / np.sqrt(DIM) / s[None, :]),
            "wq_b": bf(r(DIM) * 0.1),
            "wk_w": bf(r((DIM, DIM)) * 0.5 / np.sqrt(DIM) / s[None, :]),
            "wk_b": bf(r(DIM) * 0.1),
            "rot_re": bf(np.cos(ang)),
            "rot_im": bf(np.sin(ang))}


def reference(x, wq_w, wq_b, wk_w, wk_b, rot_re, rot_im):
    xq = mxq(f64(x), 2, "e5m2")
    q = ((xq @ mxq(f64(wq_w), 1, "e4m3").T) + f64(wq_b)).reshape(B, L, H, D)
    k = ((xq @ mxq(f64(wk_w), 1, "e4m3").T) + f64(wk_b)).reshape(B, L, H, D)
    c = f64(rot_re)[None]
    sn = f64(rot_im)[None]
    return q * c, q * sn, k * c, -(k * sn)

@@ -1,0 +1,333 @@
+from contextlib import ExitStack
+
+import concourse.mybir as mybir
+from concourse.masks import make_identity
+
+B, L, DIM = 2, 512, 1024
+FLOPS = 2 * 2 * B * L * DIM * DIM
+
+F32 = mybir.dt.float32
+BF16 = mybir.dt.bfloat16
+U32 = mybir.dt.uint32
+U8 = mybir.dt.uint8
+E5M2X4 = mybir.dt.float8_e5m2_x4
+E4M3X4 = mybir.dt.float8_e4m3fn_x4
+MULT = mybir.AluOpType.mult
+ADD = mybir.AluOpType.add
+IDENTITY = mybir.ActivationFunctionType.Identity
+
+P = 128
+PACK = 4
+PASSES = DIM // (P * PACK)
+ROWS = 4
+HALF = 512
+
+N_TIN = 8
+N_ACC = 2
+N_OUT = 4
+RES_BUFS = 11
+LOOK = 3
+PREP_CAP = 2
+KINDS = "BBBBBBBBBBBBBBBB"
+ORDER = 9
+LOADS = 0
+TIN_FIRST = True
+HEAD = 6
+WIDE = False
+LOADSEQ = "x00 q02 q12 x01 r0 k02 k12 x10 r1 x11"
+PROG = "Tx00 Tq0a Q Q B Tq0b Q Q Tq1a Q Q Tq1b Q Q M0 Q Q Tx01 Q Q M1 K0 Tk0a R0 Q Q M2a K1a Tk0b0 M2b K1b Tk0b1 Tk1a0 R1 Q Q Q M3a K2a Tk1a1 M3b K2b Tk1b R2 Q Q Q M4 K3  R3  M5 K4 Tx100 R4 Q M6 K5 Tx101 R5 Q M7 K6  R6  M8 K7  R7  M9 K8 Tx110 R8 Q Ma K9 Tx111 R9 Q Mb Ka  Ra  Mc Kb  Rb  Md Kc  Rc  Me Kd  Rd  Mf Ke  Re   Kf  Rf "
+HOLD = []
+QPOS = []
+GDELAY = 0
+GDELAY0 = 0
+QW = 1
+EARLY0 = 99
+EARLY1 = 99
+SPLIT = 99
+JOBS = "00q0B 00q1B 01q0B 01q1B 00k0B 00k1B 01k0B 01k1B 10q0B 10q1B 10k0B 10k1B 11q0B 11q1B 11k0B 11k1B"
+WP = 1
+CMAJOR = True
+FINE = 1
+PREPS = None
+MUST = 2
+QUANT_FIRST = False
+
+
+def job_order():
+    jobs = []
+    if ORDER == 0:
+        jobs = [(0, b, 0, h) for h in range(2) for b in range(B)]
+        jobs += [(0, b, 1, h) for b in range(B) for h in range(2)]
+        jobs += [(1, b, m, h) for m in range(2) for b in range(B) for h in range(2)]
+    elif ORDER == 1:
+        jobs = [(0, b, 0, h) for h in range(2) for b in range(B)]
+        for b in range(B):
+            for h in range(2):
+                jobs += [(1, b, 0, h), (0, b, 1, h)]
+        jobs += [(1, b, 1, h) for b in range(B) for h in range(2)]
+    elif ORDER == 2:
+        jobs = [(0, b, 0, h) for h in range(2) for b in range(B)]
+        jobs += [(1, b, 0, h) for b in range(B) for h in range(2)]
+        jobs += [(t, b, 1, h) for t in range(2) for b in range(B) for h in range(2)]
+    elif ORDER == 3:
+        jobs = [(0, b, 0, h) for h in range(2) for b in range(B)]
+        jobs += [(0, 0, 1, 0), (0, 0, 1, 1)]
+        jobs += [(1, 0, 0, 0), (0, 1, 1, 0), (1, 0, 0, 1), (0, 1, 1, 1)]
+        jobs += [(1, 1, 0, 0), (1, 0, 1, 0), (1, 1, 0, 1), (1, 0, 1, 1)]
+        jobs += [(1, 1, 1, 0), (1, 1, 1, 1)]
+    elif ORDER == 4:
+        jobs = [(t, b, m, h) for m in range(2) for t in range(2) for b in range(B) for h in range(2)]
+    elif ORDER == 5:
+        jobs = [(t, b, m, h) for t in range(2) for m in range(2) for b in range(B) for h in range(2)]
+    elif ORDER == 6:
+        jobs = [(t, b, 0, h) for t, b in ((0, 0), (0, 1), (1, 0)) for h in range(2)]
+        jobs += [(0, 0, 1, 0), (1, 1, 0, 0), (0, 0, 1, 1), (1, 1, 0, 1)]
+        jobs += [(t, b, 1, h) for t, b in ((0, 1), (1, 0), (1, 1)) for h in range(2)]
+    elif ORDER == 7:
+        jobs = [(0, b, m, h) for m in range(2) for b in range(B) for h in range(2)]
+        jobs += [(1, b, m, h) for b in range(B) for m in range(2) for h in range(2)]
+    elif ORDER == 9:
+        jobs = [(int(w[0]), int(w[1]), "qk".index(w[2]), int(w[3])) for w in JOBS.split()]
+    return jobs
+
+
+def tile_retention_pa_kernel(tc, x, wq_w, wq_b, wk_w, wk_b, rot_re, rot_im, out_0, out_1, out_2, out_3):
+    nc = tc.nc
+    weights, biases, rots = (wq_w, wk_w), (wq_b, wk_b), (rot_re, rot_im)
+    outs = ((out_0, out_1), (out_2, out_3))
+    jobs = job_order()
+    kind = {job: (KINDS[i] if ORDER != 9 else JOBS.split()[i][4]) for i, job in enumerate(jobs)}
+
+    with ExitStack() as ctx:
+        keep = ctx.enter_context(tc.tile_pool(name="keep", bufs=1))
+        work = ctx.enter_context(tc.tile_pool(name="work", bufs=4))
+        psum = ctx.enter_context(tc.psum_pool(name="psum", bufs=1))
+        ctx.enter_context(tc.manual_schedule())
+
+        ident = keep.tile([P, P], F32, name="ident")
+        make_identity(nc, ident[:])
+
+        bias_raw = keep.tile([16, P], BF16, name="bias_raw")
+        for m in range(2):
+            nc.scalar.dma_start(out=bias_raw[8 * m:8 * m + 8, :], in_=biases[m].rearrange("(c n) -> c n", n=P))
+
+        raw, codes, scales, rot = {}, {}, {}, {}
+
+        def load_x(t, b):
+            rows = keep.tile([P, 2 * DIM], BF16, name="x%d%d" % (t, b))
+            nc.sync.dma_start(out=rows[:], in_=x[b].rearrange("(p j) k -> p (j k)", j=ROWS)[:, 2 * t * DIM:2 * (t + 1) * DIM])
+            raw["x", t, b, 0] = rows[:]
+            codes["x", t, b] = keep.tile([P, PASSES, 2 * P], U32, name="xc%d%d" % (t, b), align_bytes=64)
+            scales["x", t, b] = keep.tile([P, PASSES, 2 * P], U8, name="xs%d%d" % (t, b), align_bytes=64)
+
+        def load_w(m, h, pieces):
+            for i in range(2):
+                src = weights[m][h * HALF + i * 2 * P:h * HALF + (i + 1) * 2 * P, :].rearrange("(p j) k -> p (j k)", j=2)
+                rows = keep.tile([P, 2 * DIM], BF16, name="w%d%d%d" % (m, h, i))
+                nc.sync.dma_start(out=rows[:], in_=src)
+                raw["w", m, h, i] = rows[:]
+            codes["w", m, h] = keep.tile([P, PASSES, HALF], U32, name="wc%d%d" % (m, h), align_bytes=64)
+            scales["w", m, h] = keep.tile([P, PASSES, HALF], U8, name="ws%d%d" % (m, h), align_bytes=64)
+
+        def load_rot(t):
+            for c in range(2):
+                rot[c, t] = keep.tile([P, 2 * DIM], BF16, name="rot%d%d" % (c, t))
+                src = rots[c].rearrange("(p j) h d -> p (j h d)", j=ROWS)
+                nc.sync.dma_start(out=rot[c, t][:], in_=src[:, 2 * t * DIM:2 * (t + 1) * DIM])
+
+        for w in LOADSEQ.split():
+            if w[0] == "x":
+                load_x(int(w[1]), int(w[2]))
+            elif w[0] == "r":
+                load_rot(int(w[1]))
+            else:
+                load_w("qk".index(w[0]), int(w[1]), int(w[2]))
+
+
+        taken = {"tin": 0, "acc": 0, "out": 0}
+        ring = {"tin": N_TIN, "acc": N_ACC, "out": N_OUT}
+
+        def bank(role):
+            role = "tin" if N_TIN == 8 or (N_ACC == 0 and role == "acc") else role
+            tag = "%s%d" % (role, taken[role] % ring[role])
+            taken[role] += 1
+            return psum.tile([P, HALF], F32, name=tag, tag=tag)
+
+        bias_wide = keep.tile([P, P], F32, name="bias_wide")
+        nc.vector.memset(bias_wide[:], 0.0)
+        nc.scalar.activation(out=bias_wide[0:16, :], in_=bias_raw[:], func=IDENTITY)
+        bias = keep.tile([P, 2, 2, ROWS], F32, name="bias")
+
+        def bias_columns():
+            bias_bank = bank("out")
+            nc.tensor.transpose(bias_bank[:, 0:P], bias_wide[:], ident[:])
+            nc.scalar.copy(out=bias[:].rearrange("a m h j -> a (m h j)"), in_=bias_bank[:, 0:16])
+
+        bias_rows = {}
+
+        def spread_bias(m, h):
+            spread = bank("out")
+            for j in range(ROWS):
+                nc.tensor.transpose(spread[:, j * P:(j + 1) * P], bias[:, m, h, j:j + 1].to_broadcast([P, P]), ident[:])
+            bias_rows[m, h] = keep.tile([P, HALF], F32, name="bias_rows%d%d" % (m, h))
+            nc.scalar.copy(out=bias_rows[m, h][:], in_=spread[:])
+
+        wide = {}
+
+        def turn(panel, pair, g):
+            words = raw[panel + (pair,)].bitcast(F32)
+            turned = bank("tin")
+            for j in range(2):
+                for u in range(2):
+                    first = j * (DIM // 2) + g * 2 * P + u
+                    nc.tensor.transpose(turned[:, (2 * j + u) * P:(2 * j + u + 1) * P], words[:, first:first - u + 2 * P:2], ident[:])
+            n = 1 if (panel, pair, g) in narrow else (2 if panel[0] == "x" else QW)
+            pos = g if panel[0] == "x" else 2 * g + pair
+            if pos % n == 0:
+                wide[panel, pos // n] = work.tile([P, n * 2 * P * PACK], BF16, name="grouped%d" % n, align_bytes=64, bufs=(4 if n == 1 else 2))
+            whole = wide[panel, pos // n]
+            grouped = whole if pos % n == n - 1 else None
+            nc.scalar.copy(
+                out=whole[:, (pos % n) * 2 * P * PACK:(pos % n + 1) * 2 * P * PACK].bitcast(F32).rearrange("a (j r u) -> a j r u" if panel[0] == "x" else "a (r j u) -> a r j u", j=2, u=2),
+                in_=turned[:].rearrange("a (j u r) -> a j r u" if panel[0] == "x" else "a (j u r) -> a r j u", j=2, u=2),
+            )
+            return grouped
+
+        def quantise(panel, pair, g, grouped):
+            if grouped is None:
+                return
+            pos = g if panel[0] == "x" else 2 * g + pair
+            cols = slice((pos + 1) * 2 * P - grouped.shape[1] // PACK, (pos + 1) * 2 * P)
+            fmt = E5M2X4 if panel[0] == "x" else E4M3X4
+            nc.vector.quantize_mx(
+                out=codes[panel][:].rearrange("a g c -> a (g c)")[:, cols].bitcast(fmt),
+                scales=scales[panel][:].rearrange("a g c -> a (g c)")[:, cols], in_=grouped[:])
+
+        staged, sums, res, begun = {}, {}, {}, set()
+        due = []
+
+        def multiply(job, part):
+            t, b, m, h = job
+            xp, wp = ("x", t, b), ("w", m, h)
+            if kind[job] in "BC":
+                if part == 0:
+                    staged[job] = work.tile([P, ROWS, 2 * P], F32, name="staged", bufs=3)
+                for jj in (part,):
+                    acc = bank("acc")
+                    for j in (2 * jj, 2 * jj + 1):
+                        ch = slice(j * P, (j + 1) * P)
+                        for g in range(PASSES):
+                            nc.tensor.matmul_mx(
+                                out=acc[:, (j % 2) * 2 * P:(j % 2 + 1) * 2 * P],
+                                lhsT=codes[wp][:, g, ch].bitcast(E4M3X4), lhsT_scale=scales[wp][:, g, ch],
+                                rhs=codes[xp][:, g, :].bitcast(E5M2X4), rhs_scale=scales[xp][:, g, :],
+                                start=(g == 0), stop=(g == PASSES - 1),
+                            )
+                    for j in (2 * jj, 2 * jj + 1):
+                        nc.scalar.activation(
+                            out=staged[job][:, j, :], in_=acc[:, (j % 2) * 2 * P:(j % 2 + 1) * 2 * P],
+                            func=IDENTITY, bias=bias[:, m, h, j:j + 1],
+                        )
+            else:
+                for s in (part,):
+                    acc = bank("acc")
+                    tok = slice(s * P, (s + 1) * P)
+                    for g in range(PASSES):
+                        nc.tensor.matmul_mx(
+                            out=acc[:],
+                            lhsT=codes[xp][:, g, tok].bitcast(E5M2X4), lhsT_scale=scales[xp][:, g, tok],
+                            rhs=codes[wp][:, g, :].bitcast(E4M3X4), rhs_scale=scales[wp][:, g, :],
+                            start=(g == 0), stop=(g == PASSES - 1),
+                        )
+                    sums[job, s] = acc
+
+        def turn_back(job, part):
+            if kind[job] not in "BC":
+                return
+            for s in (part,):
+                back = bank("out")
+                for j in range(ROWS):
+                    nc.tensor.transpose(back[:, j * P:(j + 1) * P], staged[job][:, j, s * P:(s + 1) * P], ident[:])
+                sums[job, s] = back
+
+        srcs, done = {}, {}
+
+        def add(job, s):
+            t, b, m, h = job
+            biased = work.tile([P, HALF], F32, name="biased")
+            nc.vector.tensor_tensor(out=biased[:], in0=sums[job, s][:], in1=bias_rows[m, h][:], op=ADD)
+            srcs[job, s] = biased[:]
+
+        def store(t, b, m, c, lo, hi):
+            rows = outs[m][c][b].rearrange("(p j) h d -> p (j h d)", j=ROWS)
+            nc.sync.dma_start(out=rows[:, (2 * t + lo) * DIM:(2 * t + hi) * DIM], in_=res[t, b, m, c][:, lo * DIM:hi * DIM])
+
+        def rotate(job, s, c):
+            t, b, m, h = job
+            if (t, b, m, c) not in res:
+                res[t, b, m, c] = work.tile([P, 2 * DIM], F32, name="res", bufs=RES_BUFS)
+            src = srcs[job, s] if kind[job] not in "BC" else sums[job, s][:]
+            cols = slice(s * DIM + h * HALF, s * DIM + (h + 1) * HALF)
+            dst = res[t, b, m, c][:, cols]
+            factor = rot[c, t][:, cols]
+            if kind[job] == "C" and c == 0:
+                moved = work.tile([P, HALF], F32, name="moved")
+                nc.scalar.copy(out=moved[:], in_=src)
+                nc.gpsimd.tensor_tensor(out=dst, in0=moved[:], in1=factor, op=MULT)
+            elif kind[job] == "G":
+                nc.gpsimd.tensor_tensor(out=dst, in0=src, in1=factor, op=MULT)
+            elif m == 1 and c == 1:
+                nc.vector.scalar_tensor_tensor(out=dst, in0=src, scalar=-1.0, in1=factor, op0=MULT, op1=MULT)
+            else:
+                nc.vector.tensor_tensor(out=dst, in0=src, in1=factor, op=MULT)
+            done[t, b, m, c] = done.get((t, b, m, c), 0) + 1
+            if job == jobs[-1] and (c == 1 or FINE == 2):
+                store(t, b, m, c, s, s + 1)
+            elif done[t, b, m, c] == 4 and (t, b, m) not in HOLD:
+                store(t, b, m, c, 0, 2)
+
+        narrow = []
+        made = []
+        for w in PROG.split():
+            if w[0] == "T":
+                panel = ("x", int(w[2]), int(w[3])) if w[1] == "x" else ("w", "qk".index(w[1]), int(w[2]))
+                pair = 0 if w[1] == "x" else "ab".index(w[3])
+                for g in ([int(w[4])] if len(w) > 4 else range(2)):
+                    if w[:3] != "Tx1" or not WIDE:
+                        narrow.append((panel, pair, g))
+                    made.append((panel, pair, g, turn(panel, pair, g)))
+            elif w[0] == "Q":
+                for n in range(len(w)):
+                    quantise(*made[0])
+                    made.remove(made[0])
+            elif w[0] == "B":
+                bias_columns()
+            elif w[0] == "Y":
+                for m, h in sorted({(j[2], j[3]) for j in jobs if kind[j] not in "BC"}):
+                    spread_bias(m, h)
+            elif w[0] == "S":
+                for c in range(2):
+                    store(int(w[1]), int(w[2]), "qk".index(w[3]), c, 0, 2)
+            else:
+                job = jobs[int(w[1], 16)]
+                parts = ["ab".index(w[2])] if len(w) > 2 and w[2] in "ab" else [0, 1]
+                if w[0] == "M":
+                    for part in parts:
+                        multiply(job, part)
+                elif w[0] == "K":
+                    for part in parts:
+                        turn_back(job, part)
+                elif w[0] == "A":
+                    for part in parts:
+                        add(job, part)
+                elif w[0] == "R" and w[2:] in ("r", "i"):
+                    for s in range(2):
+                        rotate(job, s, "ri".index(w[2]))
+                elif w[0] == "R":
+                    t, b, m, h = job
+                    closing = (t, b, m, 0) in res and done[t, b, m, 0] >= 2 and job != jobs[-1]
+                    closing = jobs.index((t, b, m, 1 - h)) < jobs.index(job) and job != jobs[-1]
+                    seq = [(s, c) for c in range(2) for s in range(2)] if closing else [(s, c) for s in range(2) for c in range(2)]
+                    for s, c in (seq[:2] if parts == [0] else seq[2:] if parts == [1] else seq):
+                        rotate(job, s, c)
+        assert not made

@@ -20,314 +20,234 @@ P = 128
 PACK = 4
 PASSES = DIM // (P * PACK)
 ROWS = 4
-HALF = 512
+CHUNK = 2 * P
+HALF = ROWS * P
+Q, K = 0, 1
+RE, IM = 0, 1
 
-N_TIN = 8
-N_ACC = 2
-N_OUT = 4
-RES_BUFS = 11
-LOOK = 3
-PREP_CAP = 2
-KINDS = "BBBBBBBBBBBBBBBB"
-ORDER = 9
-LOADS = 0
-TIN_FIRST = True
-HEAD = 6
-WIDE = False
-LOADSEQ = "x00 q02 q12 x01 r0 k02 k12 x10 r1 x11"
-PROG = "Tx00 Tq0a Q Q B Tq0b Q Q Tq1a Q Q Tq1b Q Q M0 Q Q Tx01 Q Q M1 K0 Tk0a R0 Q Q M2a K1a Tk0b0 M2b K1b Tk0b1 Tk1a0 R1 Q Q Q M3a K2a Tk1a1 M3b K2b Tk1b R2 Q Q Q M4 K3  R3  M5 K4 Tx100 R4 Q M6 K5 Tx101 R5 Q M7 K6  R6  M8 K7  R7  M9 K8 Tx110 R8 Q Ma K9 Tx111 R9 Q Mb Ka  Ra  Mc Kb  Rb  Md Kc  Rc  Me Kd  Rd  Mf Ke  Re   Kf  Rf "
-HOLD = []
-QPOS = []
-GDELAY = 0
-GDELAY0 = 0
-QW = 1
-EARLY0 = 99
-EARLY1 = 99
-SPLIT = 99
-JOBS = "00q0B 00q1B 01q0B 01q1B 00k0B 00k1B 01k0B 01k1B 10q0B 10q1B 10k0B 10k1B 11q0B 11q1B 11k0B 11k1B"
-WP = 1
-CMAJOR = True
-FINE = 1
-PREPS = None
-MUST = 2
-QUANT_FIRST = False
-
-
-def job_order():
-    jobs = []
-    if ORDER == 0:
-        jobs = [(0, b, 0, h) for h in range(2) for b in range(B)]
-        jobs += [(0, b, 1, h) for b in range(B) for h in range(2)]
-        jobs += [(1, b, m, h) for m in range(2) for b in range(B) for h in range(2)]
-    elif ORDER == 1:
-        jobs = [(0, b, 0, h) for h in range(2) for b in range(B)]
-        for b in range(B):
-            for h in range(2):
-                jobs += [(1, b, 0, h), (0, b, 1, h)]
-        jobs += [(1, b, 1, h) for b in range(B) for h in range(2)]
-    elif ORDER == 2:
-        jobs = [(0, b, 0, h) for h in range(2) for b in range(B)]
-        jobs += [(1, b, 0, h) for b in range(B) for h in range(2)]
-        jobs += [(t, b, 1, h) for t in range(2) for b in range(B) for h in range(2)]
-    elif ORDER == 3:
-        jobs = [(0, b, 0, h) for h in range(2) for b in range(B)]
-        jobs += [(0, 0, 1, 0), (0, 0, 1, 1)]
-        jobs += [(1, 0, 0, 0), (0, 1, 1, 0), (1, 0, 0, 1), (0, 1, 1, 1)]
-        jobs += [(1, 1, 0, 0), (1, 0, 1, 0), (1, 1, 0, 1), (1, 0, 1, 1)]
-        jobs += [(1, 1, 1, 0), (1, 1, 1, 1)]
-    elif ORDER == 4:
-        jobs = [(t, b, m, h) for m in range(2) for t in range(2) for b in range(B) for h in range(2)]
-    elif ORDER == 5:
-        jobs = [(t, b, m, h) for t in range(2) for m in range(2) for b in range(B) for h in range(2)]
-    elif ORDER == 6:
-        jobs = [(t, b, 0, h) for t, b in ((0, 0), (0, 1), (1, 0)) for h in range(2)]
-        jobs += [(0, 0, 1, 0), (1, 1, 0, 0), (0, 0, 1, 1), (1, 1, 0, 1)]
-        jobs += [(t, b, 1, h) for t, b in ((0, 1), (1, 0), (1, 1)) for h in range(2)]
-    elif ORDER == 7:
-        jobs = [(0, b, m, h) for m in range(2) for b in range(B) for h in range(2)]
-        jobs += [(1, b, m, h) for b in range(B) for m in range(2) for h in range(2)]
-    elif ORDER == 9:
-        jobs = [(int(w[0]), int(w[1]), "qk".index(w[2]), int(w[3])) for w in JOBS.split()]
-    return jobs
+RING = 4
+GROUPED_BUFS = 6
+STAGED_BUFS = 3
+BIASED_BUFS = 4
+RESULT_BUFS = 11
 
 
 def tile_retention_pa_kernel(tc, x, wq_w, wq_b, wk_w, wk_b, rot_re, rot_im, out_0, out_1, out_2, out_3):
     nc = tc.nc
     weights, biases, rots = (wq_w, wk_w), (wq_b, wk_b), (rot_re, rot_im)
     outs = ((out_0, out_1), (out_2, out_3))
-    jobs = job_order()
-    kind = {job: (KINDS[i] if ORDER != 9 else JOBS.split()[i][4]) for i, job in enumerate(jobs)}
+
+    pairs = [(0, b, m) for m in (Q, K) for b in range(B)] + [(1, b, m) for b in range(B) for m in (Q, K)]
+    x_stationary = [(0, b, Q, 0) for b in range(B)]
 
     with ExitStack() as ctx:
         keep = ctx.enter_context(tc.tile_pool(name="keep", bufs=1))
-        work = ctx.enter_context(tc.tile_pool(name="work", bufs=4))
+        work = ctx.enter_context(tc.tile_pool(name="work", bufs=1))
         psum = ctx.enter_context(tc.psum_pool(name="psum", bufs=1))
         ctx.enter_context(tc.manual_schedule())
 
         ident = keep.tile([P, P], F32, name="ident")
         make_identity(nc, ident[:])
 
-        bias_raw = keep.tile([16, P], BF16, name="bias_raw")
-        for m in range(2):
-            nc.scalar.dma_start(out=bias_raw[8 * m:8 * m + 8, :], in_=biases[m].rearrange("(c n) -> c n", n=P))
+        raw, codes, scales, rot, bias_raw = {}, {}, {}, {}, {}
 
-        raw, codes, scales, rot = {}, {}, {}, {}
+        def load_bias(m, queue):
+            bias_raw[m] = keep.tile([P, 2, ROWS], BF16, name="bias_raw%d" % m)
+            queue.dma_start(out=bias_raw[m][:], in_=biases[m].rearrange("(h p j) -> p h j", h=2, j=ROWS))
+
+        def load_operand(name, src, chunks):
+            label = "%s%d%d" % name
+            for c in range(chunks):
+                raw[name, c] = keep.tile([P, 2 * DIM], BF16, name="raw_%s_%d" % (label, c))
+                nc.sync.dma_start(out=raw[name, c][:], in_=src[:, c * 2 * DIM:(c + 1) * 2 * DIM])
+            codes[name] = keep.tile([P, PASSES, chunks * CHUNK], U32, name="codes_" + label, align_bytes=64)
+            scales[name] = keep.tile([P, PASSES, chunks * CHUNK], U8, name="scales_" + label, align_bytes=64)
 
         def load_x(t, b):
-            rows = keep.tile([P, 2 * DIM], BF16, name="x%d%d" % (t, b))
-            nc.sync.dma_start(out=rows[:], in_=x[b].rearrange("(p j) k -> p (j k)", j=ROWS)[:, 2 * t * DIM:2 * (t + 1) * DIM])
-            raw["x", t, b, 0] = rows[:]
-            codes["x", t, b] = keep.tile([P, PASSES, 2 * P], U32, name="xc%d%d" % (t, b), align_bytes=64)
-            scales["x", t, b] = keep.tile([P, PASSES, 2 * P], U8, name="xs%d%d" % (t, b), align_bytes=64)
+            rows = x[b].rearrange("(p j) k -> p (j k)", j=ROWS)
+            load_operand(("x", t, b), rows[:, t * 2 * DIM:(t + 1) * 2 * DIM], 1)
 
-        def load_w(m, h, pieces):
-            for i in range(2):
-                src = weights[m][h * HALF + i * 2 * P:h * HALF + (i + 1) * 2 * P, :].rearrange("(p j) k -> p (j k)", j=2)
-                rows = keep.tile([P, 2 * DIM], BF16, name="w%d%d%d" % (m, h, i))
-                nc.sync.dma_start(out=rows[:], in_=src)
-                raw["w", m, h, i] = rows[:]
-            codes["w", m, h] = keep.tile([P, PASSES, HALF], U32, name="wc%d%d" % (m, h), align_bytes=64)
-            scales["w", m, h] = keep.tile([P, PASSES, HALF], U8, name="ws%d%d" % (m, h), align_bytes=64)
+        def load_w(m, h):
+            load_operand(("w", m, h), weights[m][h * HALF:(h + 1) * HALF, :].rearrange("(p j) k -> p (j k)", j=ROWS), 2)
 
         def load_rot(t):
-            for c in range(2):
-                rot[c, t] = keep.tile([P, 2 * DIM], BF16, name="rot%d%d" % (c, t))
-                src = rots[c].rearrange("(p j) h d -> p (j h d)", j=ROWS)
-                nc.sync.dma_start(out=rot[c, t][:], in_=src[:, 2 * t * DIM:2 * (t + 1) * DIM])
+            for part in (RE, IM):
+                rot[part, t] = keep.tile([P, 2 * DIM], BF16, name="rot%d%d" % (part, t))
+                rows = rots[part].rearrange("(p j) h d -> p (j h d)", j=ROWS)
+                nc.sync.dma_start(out=rot[part, t][:], in_=rows[:, t * 2 * DIM:(t + 1) * 2 * DIM])
 
-        for w in LOADSEQ.split():
-            if w[0] == "x":
-                load_x(int(w[1]), int(w[2]))
-            elif w[0] == "r":
-                load_rot(int(w[1]))
-            else:
-                load_w("qk".index(w[0]), int(w[1]), int(w[2]))
+        load_bias(Q, nc.scalar)
+        load_x(0, 0)
+        load_w(Q, 0)
+        load_w(Q, 1)
+        load_x(0, 1)
+        load_rot(0)
+        load_bias(K, nc.sync)
+        load_w(K, 0)
+        load_w(K, 1)
+        load_x(1, 0)
+        load_rot(1)
+        load_x(1, 1)
 
-
-        taken = {"tin": 0, "acc": 0, "out": 0}
-        ring = {"tin": N_TIN, "acc": N_ACC, "out": N_OUT}
-
-        def bank(role):
-            role = "tin" if N_TIN == 8 or (N_ACC == 0 and role == "acc") else role
-            tag = "%s%d" % (role, taken[role] % ring[role])
-            taken[role] += 1
-            return psum.tile([P, HALF], F32, name=tag, tag=tag)
-
-        bias_wide = keep.tile([P, P], F32, name="bias_wide")
-        nc.vector.memset(bias_wide[:], 0.0)
-        nc.scalar.activation(out=bias_wide[0:16, :], in_=bias_raw[:], func=IDENTITY)
         bias = keep.tile([P, 2, 2, ROWS], F32, name="bias")
 
-        def bias_columns():
-            bias_bank = bank("out")
-            nc.tensor.transpose(bias_bank[:, 0:P], bias_wide[:], ident[:])
-            nc.scalar.copy(out=bias[:].rearrange("a m h j -> a (m h j)"), in_=bias_bank[:, 0:16])
+        def widen_bias(m):
+            nc.scalar.activation(out=bias[:, m, :, :], in_=bias_raw[m][:], func=IDENTITY)
 
-        bias_rows = {}
+        taken = {"short": 0, "long": 0}
 
-        def spread_bias(m, h):
-            spread = bank("out")
+        def bank(ring):
+            tag = "%s%d" % (ring, taken[ring] % RING)
+            taken[ring] += 1
+            return psum.tile([P, HALF], F32, name=tag, tag=tag)
+
+        bias_row = keep.tile([P, P, ROWS], F32, name="bias_row")
+
+        def spread_bias():
+            spread = bank("long")
             for j in range(ROWS):
-                nc.tensor.transpose(spread[:, j * P:(j + 1) * P], bias[:, m, h, j:j + 1].to_broadcast([P, P]), ident[:])
-            bias_rows[m, h] = keep.tile([P, HALF], F32, name="bias_rows%d%d" % (m, h))
-            nc.scalar.copy(out=bias_rows[m, h][:], in_=spread[:])
+                nc.tensor.transpose(spread[:, j * P:(j + 1) * P], bias[:, Q, 0, j:j + 1].to_broadcast([P, P]), ident[:])
+            nc.vector.tensor_copy(out=bias_row[:], in_=spread[:].rearrange("a (j p) -> a p j", j=ROWS))
 
-        wide = {}
+        waiting = []
 
-        def turn(panel, pair, g):
-            words = raw[panel + (pair,)].bitcast(F32)
-            turned = bank("tin")
-            for j in range(2):
-                for u in range(2):
-                    first = j * (DIM // 2) + g * 2 * P + u
-                    nc.tensor.transpose(turned[:, (2 * j + u) * P:(2 * j + u + 1) * P], words[:, first:first - u + 2 * P:2], ident[:])
-            n = 1 if (panel, pair, g) in narrow else (2 if panel[0] == "x" else QW)
-            pos = g if panel[0] == "x" else 2 * g + pair
-            if pos % n == 0:
-                wide[panel, pos // n] = work.tile([P, n * 2 * P * PACK], BF16, name="grouped%d" % n, align_bytes=64, bufs=(4 if n == 1 else 2))
-            whole = wide[panel, pos // n]
-            grouped = whole if pos % n == n - 1 else None
-            nc.scalar.copy(
-                out=whole[:, (pos % n) * 2 * P * PACK:(pos % n + 1) * 2 * P * PACK].bitcast(F32).rearrange("a (j r u) -> a j r u" if panel[0] == "x" else "a (r j u) -> a r j u", j=2, u=2),
-                in_=turned[:].rearrange("a (j u r) -> a j r u" if panel[0] == "x" else "a (j u r) -> a r j u", j=2, u=2),
-            )
-            return grouped
+        def turn(name, c):
+            words = raw[name, c][:].bitcast(F32)
+            for g in range(PASSES):
+                turned = bank("short")
+                for j in range(2):
+                    base = j * (DIM // 2) + g * 2 * P
+                    for u in range(2):
+                        col = (2 * j + u) * P
+                        nc.tensor.transpose(turned[:, col:col + P], words[:, base + u:base + 2 * P:2], ident[:])
+                grouped = work.tile([P, CHUNK * PACK], BF16, name="grouped", bufs=GROUPED_BUFS, align_bytes=64)
+                nc.scalar.copy(
+                    out=grouped[:].bitcast(F32).rearrange("a (j r u) -> a j r u", j=2, u=2),
+                    in_=turned[:].rearrange("a (j u r) -> a j r u", j=2, u=2),
+                )
+                waiting.append((name, c, g, grouped))
 
-        def quantise(panel, pair, g, grouped):
-            if grouped is None:
+        def quantise(chunks):
+            for name, c, g, grouped in waiting[:chunks * PASSES]:
+                cols = slice(c * CHUNK, (c + 1) * CHUNK)
+                nc.vector.quantize_mx(
+                    out=codes[name][:, g, cols].bitcast(E5M2X4 if name[0] == "x" else E4M3X4),
+                    scales=scales[name][:, g, cols],
+                    in_=grouped[:],
+                )
+                waiting.remove((name, c, g, grouped))
+
+        staged, sums, results = {}, {}, {}
+
+        def passes(out, still, still_fmt, still_cols, moving, moving_fmt):
+            for g in range(PASSES):
+                nc.tensor.matmul_mx(
+                    out=out,
+                    lhsT=codes[still][:, g, still_cols].bitcast(still_fmt),
+                    lhsT_scale=scales[still][:, g, still_cols],
+                    rhs=codes[moving][:, g, :].bitcast(moving_fmt),
+                    rhs_scale=scales[moving][:, g, :],
+                    start=(g == 0),
+                    stop=(g == PASSES - 1),
+                )
+
+        def multiply(tile):
+            t, b, m, h = tile
+            xs, ws = ("x", t, b), ("w", m, h)
+            if tile in x_stationary:
+                for s in range(2):
+                    sums[tile, s] = bank("short")
+                    passes(sums[tile, s][:], xs, E5M2X4, slice(s * P, (s + 1) * P), ws, E4M3X4)
                 return
-            pos = g if panel[0] == "x" else 2 * g + pair
-            cols = slice((pos + 1) * 2 * P - grouped.shape[1] // PACK, (pos + 1) * 2 * P)
-            fmt = E5M2X4 if panel[0] == "x" else E4M3X4
-            nc.vector.quantize_mx(
-                out=codes[panel][:].rearrange("a g c -> a (g c)")[:, cols].bitcast(fmt),
-                scales=scales[panel][:].rearrange("a g c -> a (g c)")[:, cols], in_=grouped[:])
+            staged[tile] = work.tile([P, ROWS, CHUNK], F32, name="staged", bufs=STAGED_BUFS)
+            for j0 in range(0, ROWS, 2):
+                acc = bank("short")
+                for i in range(2):
+                    passes(acc[:, i * CHUNK:(i + 1) * CHUNK], ws, E4M3X4, slice((j0 + i) * P, (j0 + i + 1) * P), xs, E5M2X4)
+                for i in range(2):
+                    nc.scalar.activation(
+                        out=staged[tile][:, j0 + i, :],
+                        in_=acc[:, i * CHUNK:(i + 1) * CHUNK],
+                        func=IDENTITY,
+                        bias=bias[:, m, h, j0 + i:j0 + i + 1],
+                    )
 
-        staged, sums, res, begun = {}, {}, {}, set()
-        due = []
+        def finish_sums(tile):
+            for s in range(2):
+                if tile in x_stationary:
+                    biased = work.tile([P, P, ROWS], F32, name="biased", bufs=BIASED_BUFS)
+                    in_bank = sums[tile, s][:].rearrange("a (j p) -> a p j", j=ROWS)
+                    nc.vector.tensor_tensor(out=biased[:], in0=in_bank, in1=bias_row[:], op=ADD)
+                    sums[tile, s] = biased[:]
+                else:
+                    back = bank("long")
+                    for j in range(ROWS):
+                        nc.tensor.transpose(back[:, j * P:(j + 1) * P], staged[tile][:, j, s * P:(s + 1) * P], ident[:])
+                    sums[tile, s] = back[:].rearrange("a (j p) -> a p j", j=ROWS)
 
-        def multiply(job, part):
-            t, b, m, h = job
-            xp, wp = ("x", t, b), ("w", m, h)
-            if kind[job] in "BC":
-                if part == 0:
-                    staged[job] = work.tile([P, ROWS, 2 * P], F32, name="staged", bufs=3)
-                for jj in (part,):
-                    acc = bank("acc")
-                    for j in (2 * jj, 2 * jj + 1):
-                        ch = slice(j * P, (j + 1) * P)
-                        for g in range(PASSES):
-                            nc.tensor.matmul_mx(
-                                out=acc[:, (j % 2) * 2 * P:(j % 2 + 1) * 2 * P],
-                                lhsT=codes[wp][:, g, ch].bitcast(E4M3X4), lhsT_scale=scales[wp][:, g, ch],
-                                rhs=codes[xp][:, g, :].bitcast(E5M2X4), rhs_scale=scales[xp][:, g, :],
-                                start=(g == 0), stop=(g == PASSES - 1),
-                            )
-                    for j in (2 * jj, 2 * jj + 1):
-                        nc.scalar.activation(
-                            out=staged[job][:, j, :], in_=acc[:, (j % 2) * 2 * P:(j % 2 + 1) * 2 * P],
-                            func=IDENTITY, bias=bias[:, m, h, j:j + 1],
-                        )
-            else:
-                for s in (part,):
-                    acc = bank("acc")
-                    tok = slice(s * P, (s + 1) * P)
-                    for g in range(PASSES):
-                        nc.tensor.matmul_mx(
-                            out=acc[:],
-                            lhsT=codes[xp][:, g, tok].bitcast(E5M2X4), lhsT_scale=scales[xp][:, g, tok],
-                            rhs=codes[wp][:, g, :].bitcast(E4M3X4), rhs_scale=scales[wp][:, g, :],
-                            start=(g == 0), stop=(g == PASSES - 1),
-                        )
-                    sums[job, s] = acc
-
-        def turn_back(job, part):
-            if kind[job] not in "BC":
-                return
-            for s in (part,):
-                back = bank("out")
-                for j in range(ROWS):
-                    nc.tensor.transpose(back[:, j * P:(j + 1) * P], staged[job][:, j, s * P:(s + 1) * P], ident[:])
-                sums[job, s] = back
-
-        srcs, done = {}, {}
-
-        def add(job, s):
-            t, b, m, h = job
-            biased = work.tile([P, HALF], F32, name="biased")
-            nc.vector.tensor_tensor(out=biased[:], in0=sums[job, s][:], in1=bias_rows[m, h][:], op=ADD)
-            srcs[job, s] = biased[:]
-
-        def store(t, b, m, c, lo, hi):
-            rows = outs[m][c][b].rearrange("(p j) h d -> p (j h d)", j=ROWS)
-            nc.sync.dma_start(out=rows[:, (2 * t + lo) * DIM:(2 * t + hi) * DIM], in_=res[t, b, m, c][:, lo * DIM:hi * DIM])
-
-        def rotate(job, s, c):
-            t, b, m, h = job
-            if (t, b, m, c) not in res:
-                res[t, b, m, c] = work.tile([P, 2 * DIM], F32, name="res", bufs=RES_BUFS)
-            src = srcs[job, s] if kind[job] not in "BC" else sums[job, s][:]
+        def product(tile, s, part):
+            t, b, m, h = tile
+            if (t, b, m, part) not in results:
+                results[t, b, m, part] = work.tile([P, 2 * DIM], F32, name="result", bufs=RESULT_BUFS)
             cols = slice(s * DIM + h * HALF, s * DIM + (h + 1) * HALF)
-            dst = res[t, b, m, c][:, cols]
-            factor = rot[c, t][:, cols]
-            if kind[job] == "C" and c == 0:
-                moved = work.tile([P, HALF], F32, name="moved")
-                nc.scalar.copy(out=moved[:], in_=src)
-                nc.gpsimd.tensor_tensor(out=dst, in0=moved[:], in1=factor, op=MULT)
-            elif kind[job] == "G":
-                nc.gpsimd.tensor_tensor(out=dst, in0=src, in1=factor, op=MULT)
-            elif m == 1 and c == 1:
-                nc.vector.scalar_tensor_tensor(out=dst, in0=src, scalar=-1.0, in1=factor, op0=MULT, op1=MULT)
+            dst = results[t, b, m, part][:, cols].rearrange("a (p j) -> a p j", j=ROWS)
+            factor = rot[part, t][:, cols].rearrange("a (p j) -> a p j", j=ROWS)
+            if m == K and part == IM:
+                nc.vector.scalar_tensor_tensor(out=dst, in0=sums[tile, s], scalar=-1.0, in1=factor, op0=MULT, op1=MULT)
             else:
-                nc.vector.tensor_tensor(out=dst, in0=src, in1=factor, op=MULT)
-            done[t, b, m, c] = done.get((t, b, m, c), 0) + 1
-            if job == jobs[-1] and (c == 1 or FINE == 2):
-                store(t, b, m, c, s, s + 1)
-            elif done[t, b, m, c] == 4 and (t, b, m) not in HOLD:
-                store(t, b, m, c, 0, 2)
+                nc.vector.tensor_tensor(out=dst, in0=sums[tile, s], in1=factor, op=MULT)
 
-        narrow = []
-        made = []
-        for w in PROG.split():
-            if w[0] == "T":
-                panel = ("x", int(w[2]), int(w[3])) if w[1] == "x" else ("w", "qk".index(w[1]), int(w[2]))
-                pair = 0 if w[1] == "x" else "ab".index(w[3])
-                for g in ([int(w[4])] if len(w) > 4 else range(2)):
-                    if w[:3] != "Tx1" or not WIDE:
-                        narrow.append((panel, pair, g))
-                    made.append((panel, pair, g, turn(panel, pair, g)))
-            elif w[0] == "Q":
-                for n in range(len(w)):
-                    quantise(*made[0])
-                    made.remove(made[0])
-            elif w[0] == "B":
-                bias_columns()
-            elif w[0] == "Y":
-                for m, h in sorted({(j[2], j[3]) for j in jobs if kind[j] not in "BC"}):
-                    spread_bias(m, h)
-            elif w[0] == "S":
-                for c in range(2):
-                    store(int(w[1]), int(w[2]), "qk".index(w[3]), c, 0, 2)
-            else:
-                job = jobs[int(w[1], 16)]
-                parts = ["ab".index(w[2])] if len(w) > 2 and w[2] in "ab" else [0, 1]
-                if w[0] == "M":
-                    for part in parts:
-                        multiply(job, part)
-                elif w[0] == "K":
-                    for part in parts:
-                        turn_back(job, part)
-                elif w[0] == "A":
-                    for part in parts:
-                        add(job, part)
-                elif w[0] == "R" and w[2:] in ("r", "i"):
-                    for s in range(2):
-                        rotate(job, s, "ri".index(w[2]))
-                elif w[0] == "R":
-                    t, b, m, h = job
-                    closing = (t, b, m, 0) in res and done[t, b, m, 0] >= 2 and job != jobs[-1]
-                    closing = jobs.index((t, b, m, 1 - h)) < jobs.index(job) and job != jobs[-1]
-                    seq = [(s, c) for c in range(2) for s in range(2)] if closing else [(s, c) for s in range(2) for c in range(2)]
-                    for s, c in (seq[:2] if parts == [0] else seq[2:] if parts == [1] else seq):
-                        rotate(job, s, c)
-        assert not made
+        def store(pair, part, first, last):
+            t, b, m = pair
+            rows = outs[m][part][b].rearrange("(p j) h d -> p (j h d)", j=ROWS)
+            nc.sync.dma_start(
+                out=rows[:, (2 * t + first) * DIM:(2 * t + last) * DIM],
+                in_=results[t, b, m, part][:, first * DIM:last * DIM],
+            )
+
+        def rotate_first(pair):
+            for s in range(2):
+                for part in (RE, IM):
+                    product(pair + (0,), s, part)
+
+        def rotate_second(pair):
+            for part in (RE, IM):
+                by_row = pair == pairs[-1] and part == IM
+                for s in range(2):
+                    product(pair + (1,), s, part)
+                    if by_row:
+                        store(pair, part, s, s + 1)
+                if not by_row:
+                    store(pair, part, 0, 2)
+
+        def halves(m, h):
+            return [(("w", m, h), c) for c in range(2)]
+
+        widen_bias(Q)
+        head = [(("x", 0, 0), 0)] + halves(Q, 0) + halves(Q, 1)
+        for i, (name, c) in enumerate(head):
+            if i == 2:
+                spread_bias()
+            turn(name, c)
+            if i > 0:
+                quantise(1)
+        quantise(1)
+
+        between = {0: [(("x", 0, 1), 0)], 1: halves(K, 1), 2: [(("x", 1, 0), 0)], 4: [(("x", 1, 1), 0)]}
+        after = {0: halves(K, 0)}
+
+        for i, pair in enumerate(pairs):
+            multiply(pair + (0,))
+            multiply(pair + (1,))
+            if i == 1:
+                widen_bias(K)
+            finish_sums(pair + (0,))
+            for name, c in between.get(i, []):
+                turn(name, c)
+            finish_sums(pair + (1,))
+            for name, c in after.get(i, []):
+                turn(name, c)
+            rotate_first(pair)
+            quantise(len(between.get(i, [])))
+            rotate_second(pair)
+            quantise(len(after.get(i, [])))

from contextlib import ExitStack

import concourse.mybir as mybir
from concourse.masks import make_identity

B, L, DIM = 2, 512, 1024
FLOPS = 2 * 2 * B * L * DIM * DIM

F32 = mybir.dt.float32
BF16 = mybir.dt.bfloat16
U32 = mybir.dt.uint32
U8 = mybir.dt.uint8
E5M2X4 = mybir.dt.float8_e5m2_x4
E4M3X4 = mybir.dt.float8_e4m3fn_x4
MULT = mybir.AluOpType.mult
ADD = mybir.AluOpType.add
IDENTITY = mybir.ActivationFunctionType.Identity

P = 128
PACK = 4
PASSES = DIM // (P * PACK)
ROWS = 4
CHUNK = 2 * P
HALF = ROWS * P
Q, K = 0, 1
RE, IM = 0, 1

RING = 4
GROUPED_BUFS = 6
STAGED_BUFS = 3
BIASED_BUFS = 4
RESULT_BUFS = 11


def tile_retention_pa_kernel(tc, x, wq_w, wq_b, wk_w, wk_b, rot_re, rot_im, out_0, out_1, out_2, out_3):
    nc = tc.nc
    weights, biases, rots = (wq_w, wk_w), (wq_b, wk_b), (rot_re, rot_im)
    outs = ((out_0, out_1), (out_2, out_3))

    pairs = [(0, b, m) for m in (Q, K) for b in range(B)] + [(1, b, m) for b in range(B) for m in (Q, K)]
    x_stationary = [(0, b, Q, 0) for b in range(B)]

    with ExitStack() as ctx:
        keep = ctx.enter_context(tc.tile_pool(name="keep", bufs=1))
        work = ctx.enter_context(tc.tile_pool(name="work", bufs=1))
        psum = ctx.enter_context(tc.psum_pool(name="psum", bufs=1))
        ctx.enter_context(tc.manual_schedule())

        ident = keep.tile([P, P], F32, name="ident")
        make_identity(nc, ident[:])

        raw, codes, scales, rot, bias_raw = {}, {}, {}, {}, {}

        def load_bias(m, queue):
            bias_raw[m] = keep.tile([P, 2, ROWS], BF16, name="bias_raw%d" % m)
            queue.dma_start(out=bias_raw[m][:], in_=biases[m].rearrange("(h p j) -> p h j", h=2, j=ROWS))

        def load_operand(name, src, chunks):
            label = "%s%d%d" % name
            for c in range(chunks):
                raw[name, c] = keep.tile([P, 2 * DIM], BF16, name="raw_%s_%d" % (label, c))
                nc.sync.dma_start(out=raw[name, c][:], in_=src[:, c * 2 * DIM:(c + 1) * 2 * DIM])
            codes[name] = keep.tile([P, PASSES, chunks * CHUNK], U32, name="codes_" + label, align_bytes=64)
            scales[name] = keep.tile([P, PASSES, chunks * CHUNK], U8, name="scales_" + label, align_bytes=64)

        def load_x(t, b):
            rows = x[b].rearrange("(p j) k -> p (j k)", j=ROWS)
            load_operand(("x", t, b), rows[:, t * 2 * DIM:(t + 1) * 2 * DIM], 1)

        def load_w(m, h):
            load_operand(("w", m, h), weights[m][h * HALF:(h + 1) * HALF, :].rearrange("(p j) k -> p (j k)", j=ROWS), 2)

        def load_rot(t):
            for part in (RE, IM):
                rot[part, t] = keep.tile([P, 2 * DIM], BF16, name="rot%d%d" % (part, t))
                rows = rots[part].rearrange("(p j) h d -> p (j h d)", j=ROWS)
                nc.sync.dma_start(out=rot[part, t][:], in_=rows[:, t * 2 * DIM:(t + 1) * 2 * DIM])

        load_bias(Q, nc.scalar)
        load_x(0, 0)
        load_w(Q, 0)
        load_w(Q, 1)
        load_x(0, 1)
        load_rot(0)
        load_bias(K, nc.sync)
        load_w(K, 0)
        load_w(K, 1)
        load_x(1, 0)
        load_rot(1)
        load_x(1, 1)

        bias = keep.tile([P, 2, 2, ROWS], F32, name="bias")

        def widen_bias(m):
            nc.scalar.activation(out=bias[:, m, :, :], in_=bias_raw[m][:], func=IDENTITY)

        taken = {"short": 0, "long": 0}

        def bank(ring):
            tag = "%s%d" % (ring, taken[ring] % RING)
            taken[ring] += 1
            return psum.tile([P, HALF], F32, name=tag, tag=tag)

        bias_row = keep.tile([P, P, ROWS], F32, name="bias_row")

        def spread_bias():
            spread = bank("long")
            for j in range(ROWS):
                nc.tensor.transpose(spread[:, j * P:(j + 1) * P], bias[:, Q, 0, j:j + 1].to_broadcast([P, P]), ident[:])
            nc.vector.tensor_copy(out=bias_row[:], in_=spread[:].rearrange("a (j p) -> a p j", j=ROWS))

        waiting = []

        def turn(name, c):
            words = raw[name, c][:].bitcast(F32)
            for g in range(PASSES):
                turned = bank("short")
                for j in range(2):
                    base = j * (DIM // 2) + g * 2 * P
                    for u in range(2):
                        col = (2 * j + u) * P
                        nc.tensor.transpose(turned[:, col:col + P], words[:, base + u:base + 2 * P:2], ident[:])
                grouped = work.tile([P, CHUNK * PACK], BF16, name="grouped", bufs=GROUPED_BUFS, align_bytes=64)
                nc.scalar.copy(
                    out=grouped[:].bitcast(F32).rearrange("a (j r u) -> a j r u", j=2, u=2),
                    in_=turned[:].rearrange("a (j u r) -> a j r u", j=2, u=2),
                )
                waiting.append((name, c, g, grouped))

        def quantise(chunks):
            for name, c, g, grouped in waiting[:chunks * PASSES]:
                cols = slice(c * CHUNK, (c + 1) * CHUNK)
                nc.vector.quantize_mx(
                    out=codes[name][:, g, cols].bitcast(E5M2X4 if name[0] == "x" else E4M3X4),
                    scales=scales[name][:, g, cols],
                    in_=grouped[:],
                )
                waiting.remove((name, c, g, grouped))

        staged, sums, results = {}, {}, {}

        def passes(out, still, still_fmt, still_cols, moving, moving_fmt):
            for g in range(PASSES):
                nc.tensor.matmul_mx(
                    out=out,
                    lhsT=codes[still][:, g, still_cols].bitcast(still_fmt),
                    lhsT_scale=scales[still][:, g, still_cols],
                    rhs=codes[moving][:, g, :].bitcast(moving_fmt),
                    rhs_scale=scales[moving][:, g, :],
                    start=(g == 0),
                    stop=(g == PASSES - 1),
                )

        def multiply(tile):
            t, b, m, h = tile
            xs, ws = ("x", t, b), ("w", m, h)
            if tile in x_stationary:
                for s in range(2):
                    sums[tile, s] = bank("short")
                    passes(sums[tile, s][:], xs, E5M2X4, slice(s * P, (s + 1) * P), ws, E4M3X4)
                return
            staged[tile] = work.tile([P, ROWS, CHUNK], F32, name="staged", bufs=STAGED_BUFS)
            for j0 in range(0, ROWS, 2):
                acc = bank("short")
                for i in range(2):
                    passes(acc[:, i * CHUNK:(i + 1) * CHUNK], ws, E4M3X4, slice((j0 + i) * P, (j0 + i + 1) * P), xs, E5M2X4)
                for i in range(2):
                    nc.scalar.activation(
                        out=staged[tile][:, j0 + i, :],
                        in_=acc[:, i * CHUNK:(i + 1) * CHUNK],
                        func=IDENTITY,
                        bias=bias[:, m, h, j0 + i:j0 + i + 1],
                    )

        def finish_sums(tile):
            for s in range(2):
                if tile in x_stationary:
                    biased = work.tile([P, P, ROWS], F32, name="biased", bufs=BIASED_BUFS)
                    in_bank = sums[tile, s][:].rearrange("a (j p) -> a p j", j=ROWS)
                    nc.vector.tensor_tensor(out=biased[:], in0=in_bank, in1=bias_row[:], op=ADD)
                    sums[tile, s] = biased[:]
                else:
                    back = bank("long")
                    for j in range(ROWS):
                        nc.tensor.transpose(back[:, j * P:(j + 1) * P], staged[tile][:, j, s * P:(s + 1) * P], ident[:])
                    sums[tile, s] = back[:].rearrange("a (j p) -> a p j", j=ROWS)

        def product(tile, s, part):
            t, b, m, h = tile
            if (t, b, m, part) not in results:
                results[t, b, m, part] = work.tile([P, 2 * DIM], F32, name="result", bufs=RESULT_BUFS)
            cols = slice(s * DIM + h * HALF, s * DIM + (h + 1) * HALF)
            dst = results[t, b, m, part][:, cols].rearrange("a (p j) -> a p j", j=ROWS)
            factor = rot[part, t][:, cols].rearrange("a (p j) -> a p j", j=ROWS)
            if m == K and part == IM:
                nc.vector.scalar_tensor_tensor(out=dst, in0=sums[tile, s], scalar=-1.0, in1=factor, op0=MULT, op1=MULT)
            else:
                nc.vector.tensor_tensor(out=dst, in0=sums[tile, s], in1=factor, op=MULT)

        def store(pair, part, first, last):
            t, b, m = pair
            rows = outs[m][part][b].rearrange("(p j) h d -> p (j h d)", j=ROWS)
            nc.sync.dma_start(
                out=rows[:, (2 * t + first) * DIM:(2 * t + last) * DIM],
                in_=results[t, b, m, part][:, first * DIM:last * DIM],
            )

        def rotate_first(pair):
            for s in range(2):
                for part in (RE, IM):
                    product(pair + (0,), s, part)

        def rotate_second(pair):
            for part in (RE, IM):
                by_row = pair == pairs[-1] and part == IM
                for s in range(2):
                    product(pair + (1,), s, part)
                    if by_row:
                        store(pair, part, s, s + 1)
                if not by_row:
                    store(pair, part, 0, 2)

        def halves(m, h):
            return [(("w", m, h), c) for c in range(2)]

        widen_bias(Q)
        head = [(("x", 0, 0), 0)] + halves(Q, 0) + halves(Q, 1)
        for i, (name, c) in enumerate(head):
            if i == 2:
                spread_bias()
            turn(name, c)
            if i > 0:
                quantise(1)
        quantise(1)

        between = {0: [(("x", 0, 1), 0)], 1: halves(K, 1), 2: [(("x", 1, 0), 0)], 4: [(("x", 1, 1), 0)]}
        after = {0: halves(K, 0)}

        for i, pair in enumerate(pairs):
            multiply(pair + (0,))
            multiply(pair + (1,))
            if i == 1:
                widen_bias(K)
            finish_sums(pair + (0,))
            for name, c in between.get(i, []):
                turn(name, c)
            finish_sums(pair + (1,))
            for name, c in after.get(i, []):
                turn(name, c)
            rotate_first(pair)
            quantise(len(between.get(i, [])))
            rotate_second(pair)
            quantise(len(after.get(i, [])))
